import numpy as np
import ml_dtypes


def mxq(x, axis, fmt="e4m3"):
    dtype, down = {"e4m3": (ml_dtypes.float8_e4m3fn, 7), "e5m2": (ml_dtypes.float8_e5m2, 14)}[fmt]
    v = np.moveaxis(np.asarray(x, np.float32).astype(ml_dtypes.bfloat16).astype(np.float64), axis, -1)
    blocks = v.reshape(v.shape[:-1] + (-1, 32))
    amax = np.abs(blocks).max(-1, keepdims=True)
    byte = np.maximum(np.where(amax > 0, np.frexp(amax)[1] - 1 + 127, 0) - down, 1)
    scale = np.exp2(byte - 127.0)
    codes = (blocks / scale).astype(np.float32).astype(dtype).astype(np.float64)
    return np.moveaxis((codes * scale).reshape(v.shape), -1, axis)


WIDE = False


def mx_kscale(k):
    if not WIDE:
        return np.ones(k)
    levels = np.array([10, -10, 5, -5, 0])
    a = np.random.permutation(np.resize(levels, k // 512 * 4)).reshape(k // 512, 4)
    idx = np.arange(k)
    return np.exp2(a[idx // 512, idx % 128 // 32])


BF16 = ml_dtypes.bfloat16


def bf(x):
    return np.asarray(x, np.float32).astype(BF16)


def f64(x):
    return np.asarray(x).astype(np.float64)


B, N, LD, HID = 16, 255, 1024, 512
NE = N + 1
DT, DX = 5e-4, 1e-3
FLUX_SCALE = 0.25
EH = 0.5
ET = 13


def erfc_pos(a):
    a = np.minimum(a, 9.0)
    acc = np.zeros_like(a)
    for n in range(ET):
        t2 = ((n + 0.5) * EH) ** 2
        acc += np.exp(-t2) / (t2 + a * a)
    return 2.0 * EH * a * np.exp(-a * a) / np.pi * acc + 2.0 / (1.0 + np.exp(2.0 * np.pi * a / EH))


def erf(z):
    return np.sign(z) * (1.0 - erfc_pos(np.abs(z)))


def gelu(v):
    return 0.5 * v * (1.0 + erf(v / np.sqrt(2.0)))


def setup_inputs():
    s = mx_kscale(HID)
    return {"edge_hid": bf(gelu(np.random.standard_normal((B, NE, HID)) * 1.4) * s),
            "u": bf(np.random.random((B, N))),
            "enc": bf((1.0 + 0.5 * np.random.standard_normal(LD)) / np.sqrt(LD)),
            "W2": bf(np.random.standard_normal((HID, HID)) * 1.2 / np.sqrt(HID) / s[:, None]),
            "b2": bf(np.random.standard_normal(HID) * 0.5),
            "W3": bf(np.random.standard_normal((HID, LD)) * 1.8 / np.sqrt(HID)),
            "b3": bf(np.random.standard_normal(LD) * 0.5)}


def reference(edge_hid, u, enc, W2, b2, W3, b3):
    u, enc = f64(u), f64(enc)
    h = u[..., None] * enc
    x = gelu((mxq(f64(edge_hid), 2, "e4m3") @ mxq(f64(W2), 0, "e4m3")) + f64(b2))
    flux = np.tanh((mxq(x, 2, "e4m3") @ mxq(f64(W3), 0, "e4m3")) + f64(b3)) * FLUX_SCALE
    h_new = h - (DT / DX) * (flux[:, 1:] - flux[:, :-1])
    dec = enc / (np.sum(enc * enc) + 1e-12)
    return np.sum(h_new * dec, axis=-1)

@@ -1,0 +1,265 @@
+from contextlib import ExitStack
+
+import concourse.mybir as mybir
+from concourse.masks import make_identity
+
+F32 = mybir.dt.float32
+BF16 = mybir.dt.bfloat16
+U32 = mybir.dt.uint32
+U8 = mybir.dt.uint8
+FP8X4 = mybir.dt.float8_e4m3fn_x4
+ACT = mybir.ActivationFunctionType
+ALU = mybir.AluOpType
+AXIS = mybir.AxisListType
+
+P = 128
+PACK = 4
+GRIDS = 16
+FACES = 256
+CELLS = FACES - 1
+HID = 512
+LATENT = 1024
+GROUP = 512
+N_GROUPS = GRIDS * FACES // GROUP
+GRIDS_PER_GROUP = GROUP // FACES
+HID_TILES = HID // P
+LATENT_TILES = LATENT // P
+CHAINS = 2
+FLUX_WEIGHT = 0.125
+B2_ROW = 0
+B3_ROW = B2_ROW + HID_TILES
+ENC_ROW = B3_ROW + LATENT_TILES
+VEC_ROWS = ENC_ROW + LATENT_TILES
+
+FLOPS = 2 * GRIDS * FACES * HID * (HID + LATENT)
+
+
+def regroup(nc, grouped, planes):
+    nc.vector.tensor_copy(
+        out=grouped.rearrange("p (c i t) -> p c t i", i=4, t=PACK),
+        in_=planes.rearrange("p t (c i) -> p c t i", i=4),
+    )
+
+
+def quantise(nc, codes, scales, grouped):
+    nc.vector.quantize_mx(out=codes.bitcast(FP8X4), scales=scales, in_=grouped)
+
+
+def tile_fluxgnn1dlatent_pb_t_kernel(tc, edge_hid, u, enc, W2, b2, W3, b3, out):
+    nc = tc.nc
+    with ExitStack() as stack:
+        const = stack.enter_context(tc.tile_pool(name="const", bufs=1))
+        edge_pool = stack.enter_context(tc.tile_pool(name="edge", bufs=N_GROUPS))
+        stage = stack.enter_context(tc.tile_pool(name="stage", bufs=2))
+        tanh_pool = stack.enter_context(tc.tile_pool(name="tanh", bufs=4))
+        psum_tp = stack.enter_context(tc.psum_pool(name="psum_tp", bufs=2))
+        psum_z = stack.enter_context(tc.psum_pool(name="psum_z", bufs=5))
+        psum_g = stack.enter_context(tc.psum_pool(name="psum_g", bufs=1))
+
+        vec_rows = const.tile([P, P], BF16)
+        nc.vector.memset(vec_rows[:], 0.0)
+        nc.scalar.dma_start(out=vec_rows[B2_ROW:B3_ROW, :], in_=b2.rearrange("(t p) -> t p", p=P))
+        nc.scalar.dma_start(out=vec_rows[B3_ROW:ENC_ROW, :], in_=b3.rearrange("(t p) -> t p", p=P))
+        nc.scalar.dma_start(out=vec_rows[ENC_ROW:VEC_ROWS, :], in_=enc.rearrange("(t p) -> t p", p=P))
+        u_bf = const.tile([GRIDS, CELLS], BF16)
+        nc.scalar.dma_start(out=u_bf[:], in_=u)
+
+        w2_planes = const.tile([P, PACK, HID], BF16)
+        nc.sync.dma_start(
+            out=w2_planes[:].rearrange("p (h e) c -> p h e c", e=2),
+            in_=W2.rearrange("(h p e) c -> p h e c", h=2, e=2),
+        )
+        edge_view = edge_hid.flatten_outer_dims().rearrange("(g s p) k -> g p s k", s=GROUP // P, p=P)
+        edge_tiles = []
+        w3_planes = const.tile([P, PACK, LATENT], BF16)
+        for g in range(N_GROUPS):
+            edge_rows = edge_pool.tile([P, (GROUP // P) * HID], BF16, tag="edge")
+            nc.sync.dma_start(out=edge_rows[:].rearrange("p (s k) -> p s k", k=HID), in_=edge_view[g])
+            edge_tiles.append(edge_rows)
+            if g == 1:
+                nc.sync.dma_start(out=w3_planes[:], in_=W3.rearrange("(t p) c -> p t c", p=P))
+
+        ident_f32 = const.tile([P, P], F32)
+        make_identity(nc, ident_f32[:])
+        ident_bf = const.tile([P, P], BF16)
+        make_identity(nc, ident_bf[:])
+        ones = const.tile([P, P], F32)
+        nc.vector.memset(ones[:], 1.0)
+        window = const.tile([P, 2 * P], F32)
+        nc.vector.memset(window[:], 0.0)
+        nc.vector.memset(window[:, P : P + 1], 1.0)
+        warm = const.tile([P, 1], F32)
+        nc.scalar.activation(out=warm[:], in_=ones[:, 0:1], func=ACT.Gelu)
+
+        w2_grouped = const.tile([P, HID * PACK], BF16, align_bytes=64)
+        w2_codes = const.tile([P, HID], U32, align_bytes=64)
+        w2_scales = const.tile([P, HID], U8, align_bytes=64)
+        w3_grouped = const.tile([P, LATENT * PACK], BF16, align_bytes=64)
+        w3_codes = const.tile([P, LATENT], U32, align_bytes=64)
+        w3_scales = const.tile([P, LATENT], U8, align_bytes=64)
+
+        edge_codes = {}
+        edge_grouped = {}
+        x_planes = {}
+        x_grouped = {}
+        x_codes = {}
+        sums = {}
+
+        def transpose_edge(g):
+            words = edge_tiles[g][:].bitcast(F32)
+            grouped = stage.tile([P, GROUP * PACK], BF16, tag="edge_grouped", align_bytes=64)
+            grouped_words = grouped[:].bitcast(F32).rearrange("p (r h) -> p r h", h=2)
+            for half in range(2):
+                tp = psum_tp.tile([P, 2, FACES], F32, tag="tp")
+                for s in range(2):
+                    for h in range(2):
+                        first = (2 * half + s) * (HID // 2) + h * P
+                        nc.tensor.transpose(
+                            tp[:, h, s * P : (s + 1) * P], words[:, first : first + P], ident_f32[:]
+                        )
+                dst = grouped_words[:, half * FACES : (half + 1) * FACES, :]
+                src = tp[:].rearrange("p h r -> p r h")
+                if half == 0:
+                    nc.vector.tensor_copy(out=dst, in_=src)
+                else:
+                    nc.scalar.copy(out=dst, in_=src)
+            edge_grouped[g] = grouped
+
+        def quantise_edge(g):
+            codes = stage.tile([P, GROUP], U32, tag="edge_codes", align_bytes=64)
+            scales = stage.tile([P, GROUP], U8, tag="edge_scales", align_bytes=64)
+            quantise(nc, codes[:], scales[:], edge_grouped[g][:])
+            edge_codes[g] = (codes, scales)
+
+        def layer1(g):
+            codes, scales = edge_codes[g]
+            planes = stage.tile([P, PACK, GROUP], BF16, tag="x_planes")
+            for t in range(HID_TILES):
+                cols = slice(t * P, (t + 1) * P)
+                z = psum_z.tile([P, GROUP], F32, tag="z")
+                nc.tensor.matmul_mx(
+                    out=z[:],
+                    lhsT=w2_codes[:, cols].bitcast(FP8X4),
+                    lhsT_scale=w2_scales[:, cols],
+                    rhs=codes[:].bitcast(FP8X4),
+                    rhs_scale=scales[:],
+                    start=True,
+                    stop=True,
+                )
+                nc.scalar.activation(
+                    out=planes[:, t, :], in_=z[:], func=ACT.Gelu, bias=vec_cols[:, B2_ROW + t : B2_ROW + t + 1]
+                )
+            x_planes[g] = planes
+
+        def regroup_x(g):
+            grouped = stage.tile([P, GROUP * PACK], BF16, tag="x_grouped", align_bytes=64)
+            regroup(nc, grouped[:], x_planes[g][:])
+            x_grouped[g] = grouped
+
+        def quantise_x(g):
+            codes = stage.tile([P, GROUP], U32, tag="x_codes", align_bytes=64)
+            scales = stage.tile([P, GROUP], U8, tag="x_scales", align_bytes=64)
+            quantise(nc, codes[:], scales[:], x_grouped[g][:])
+            x_codes[g] = (codes, scales)
+
+        def layer2_tile(g, j):
+            codes, scales = x_codes[g]
+            cols = slice(j * P, (j + 1) * P)
+            z = psum_z.tile([P, GROUP], F32, tag="z")
+            nc.tensor.matmul_mx(
+                out=z[:],
+                lhsT=w3_codes[:, cols].bitcast(FP8X4),
+                lhsT_scale=w3_scales[:, cols],
+                rhs=codes[:].bitcast(FP8X4),
+                rhs_scale=scales[:],
+                start=True,
+                stop=True,
+            )
+            flux = tanh_pool.tile([P, GROUP], F32, tag="flux")
+            nc.scalar.activation(
+                out=flux[:], in_=z[:], func=ACT.Tanh, bias=vec_cols[:, B3_ROW + j : B3_ROW + j + 1]
+            )
+            if j < CHAINS:
+                partial = stage.tile([P, GROUP], F32, tag="sum%d" % j)
+                nc.vector.tensor_scalar_mul(out=partial[:], in0=flux[:], scalar1=weight[:, j : j + 1])
+                sums[(g, j)] = partial
+            else:
+                partial = sums[(g, j % CHAINS)]
+                nc.vector.scalar_tensor_tensor(
+                    out=partial[:],
+                    in0=flux[:],
+                    scalar=weight[:, j : j + 1],
+                    in1=partial[:],
+                    op0=ALU.mult,
+                    op1=ALU.add,
+                )
+
+        def reduce_partitions(g):
+            for grid in range(GRIDS_PER_GROUP):
+                b = g * GRIDS_PER_GROUP + grid
+                for chain in range(CHAINS):
+                    nc.tensor.matmul(
+                        out=g_sum[:],
+                        lhsT=window[:, P - b : 2 * P - b],
+                        rhs=sums[(g, chain)][:, grid * FACES : (grid + 1) * FACES],
+                        start=(b == 0 and chain == 0),
+                        stop=(b == GRIDS - 1 and chain == CHAINS - 1),
+                    )
+
+        regroup(nc, w2_grouped[:], w2_planes[:])
+        transpose_edge(0)
+        quantise(nc, w2_codes[:], w2_scales[:], w2_grouped[:])
+        quantise_edge(0)
+
+        vec_ps = psum_tp.tile([P, P], BF16, tag="tp")
+        nc.tensor.transpose(vec_ps[:], vec_rows[:], ident_bf[:])
+        vec_cols = const.tile([P, VEC_ROWS], F32)
+        nc.vector.tensor_copy(out=vec_cols[:], in_=vec_ps[:, 0:VEC_ROWS])
+        enc_cols = vec_cols[:, ENC_ROW:VEC_ROWS]
+        enc_sq = const.tile([P, LATENT_TILES], F32)
+        nc.vector.tensor_tensor(out=enc_sq[:], in0=enc_cols, in1=enc_cols, op=ALU.mult)
+        s_ps = psum_tp.tile([P, LATENT_TILES], F32, tag="tp")
+        nc.tensor.matmul(out=s_ps[:], lhsT=ones[:], rhs=enc_sq[:], start=True, stop=True)
+        s_sum = const.tile([P, 1], F32)
+        nc.vector.reduce_sum(out=s_sum[:], in_=s_ps[:], axis=AXIS.X)
+        s_eps = const.tile([P, 1], F32)
+        nc.vector.tensor_scalar_add(out=s_eps[:], in0=s_sum[:], scalar1=1e-12)
+        s_inv = const.tile([P, 1], F32)
+        nc.vector.reciprocal(out=s_inv[:], in_=s_eps[:])
+        weight = const.tile([P, LATENT_TILES], F32)
+        nc.vector.tensor_scalar(
+            out=weight[:], in0=enc_cols, scalar1=s_inv[:, 0:1], scalar2=FLUX_WEIGHT, op0=ALU.mult, op1=ALU.mult
+        )
+        u_gain = const.tile([P, 1], F32)
+        nc.vector.tensor_tensor(out=u_gain[:], in0=s_sum[:], in1=s_inv[:], op=ALU.mult)
+        u_term = const.tile([GRIDS, CELLS], F32)
+        nc.vector.tensor_scalar_mul(out=u_term[:], in0=u_bf[:], scalar1=u_gain[0:GRIDS, 0:1])
+
+        g_sum = psum_g.tile([P, FACES], F32)
+
+        for g in range(-1, N_GROUPS + 1):
+            if g + 1 < N_GROUPS:
+                layer1(g + 1)
+            if g + 2 < N_GROUPS:
+                transpose_edge(g + 2)
+            if g == -1:
+                regroup(nc, w3_grouped[:], w3_planes[:])
+            if g + 1 < N_GROUPS:
+                regroup_x(g + 1)
+            if g + 2 < N_GROUPS:
+                quantise_edge(g + 2)
+            if g == -1:
+                quantise(nc, w3_codes[:], w3_scales[:], w3_grouped[:])
+            for j in range(LATENT_TILES):
+                if j == CHAINS and g + 1 < N_GROUPS:
+                    quantise_x(g + 1)
+                if 0 <= g < N_GROUPS:
+                    layer2_tile(g, j)
+            if g >= 1:
+                reduce_partitions(g - 1)
+
+        left = const.tile([GRIDS, CELLS], F32)
+        nc.vector.tensor_tensor(out=left[:], in0=u_term[:], in1=g_sum[0:GRIDS, 0:CELLS], op=ALU.add)
+        result = const.tile([GRIDS, CELLS], F32)
+        nc.vector.tensor_tensor(out=result[:], in0=left[:], in1=g_sum[0:GRIDS, 1:FACES], op=ALU.subtract)
+        nc.sync.dma_start(out=out, in_=result[:])

@@ -25,6 +25,9 @@ GRIDS_PER_GROUP = GROUP // FACES
 HID_TILES = HID // P
 LATENT_TILES = LATENT // P
 CHAINS = 2
+Z_BANKS = 5
+W3_PARTS = 2
+W3_PART = LATENT // W3_PARTS
 FLUX_WEIGHT = 0.125
 B2_ROW = 0
 B3_ROW = B2_ROW + HID_TILES
@@ -51,10 +54,11 @@ def tile_fluxgnn1dlatent_pb_t_kernel(tc, edge_hid, u, enc, W2, b2, W3, b3, out):
         const = stack.enter_context(tc.tile_pool(name="const", bufs=1))
         edge_pool = stack.enter_context(tc.tile_pool(name="edge", bufs=N_GROUPS))
         stage = stack.enter_context(tc.tile_pool(name="stage", bufs=2))
-        tanh_pool = stack.enter_context(tc.tile_pool(name="tanh", bufs=4))
+        tanh_pool = stack.enter_context(tc.tile_pool(name="tanh", bufs=LATENT_TILES))
         psum_tp = stack.enter_context(tc.psum_pool(name="psum_tp", bufs=2))
-        psum_z = stack.enter_context(tc.psum_pool(name="psum_z", bufs=5))
+        psum_z = stack.enter_context(tc.psum_pool(name="psum_z", bufs=Z_BANKS))
         psum_g = stack.enter_context(tc.psum_pool(name="psum_g", bufs=1))
+        stack.enter_context(tc.manual_schedule())
 
         vec_rows = const.tile([P, P], BF16)
         nc.vector.memset(vec_rows[:], 0.0)
@@ -79,10 +83,10 @@ def tile_fluxgnn1dlatent_pb_t_kernel(tc, edge_hid, u, enc, W2, b2, W3, b3, out):
             if g == 1:
                 nc.sync.dma_start(out=w3_planes[:], in_=W3.rearrange("(t p) c -> p t c", p=P))
 
-        ident_f32 = const.tile([P, P], F32)
-        make_identity(nc, ident_f32[:])
         ident_bf = const.tile([P, P], BF16)
         make_identity(nc, ident_bf[:])
+        ident_f32 = const.tile([P, P], F32)
+        make_identity(nc, ident_f32[:])
         ones = const.tile([P, P], F32)
         nc.vector.memset(ones[:], 1.0)
         window = const.tile([P, 2 * P], F32)
@@ -105,7 +109,7 @@ def tile_fluxgnn1dlatent_pb_t_kernel(tc, edge_hid, u, enc, W2, b2, W3, b3, out):
         x_codes = {}
         sums = {}
 
-        def transpose_edge(g):
+        def transpose_edge(g, vector_halves):
             words = edge_tiles[g][:].bitcast(F32)
             grouped = stage.tile([P, GROUP * PACK], BF16, tag="edge_grouped", align_bytes=64)
             grouped_words = grouped[:].bitcast(F32).rearrange("p (r h) -> p r h", h=2)
@@ -119,7 +123,7 @@ def tile_fluxgnn1dlatent_pb_t_kernel(tc, edge_hid, u, enc, W2, b2, W3, b3, out):
                         )
                 dst = grouped_words[:, half * FACES : (half + 1) * FACES, :]
                 src = tp[:].rearrange("p h r -> p r h")
-                if half == 0:
+                if half < vector_halves:
                     nc.vector.tensor_copy(out=dst, in_=src)
                 else:
                     nc.scalar.copy(out=dst, in_=src)
@@ -195,9 +199,9 @@ def tile_fluxgnn1dlatent_pb_t_kernel(tc, edge_hid, u, enc, W2, b2, W3, b3, out):
                 )
 
         def reduce_partitions(g):
-            for grid in range(GRIDS_PER_GROUP):
-                b = g * GRIDS_PER_GROUP + grid
-                for chain in range(CHAINS):
+            for chain in range(CHAINS):
+                for grid in range(GRIDS_PER_GROUP):
+                    b = g * GRIDS_PER_GROUP + grid
                     nc.tensor.matmul(
                         out=g_sum[:],
                         lhsT=window[:, P - b : 2 * P - b],
@@ -206,19 +210,34 @@ def tile_fluxgnn1dlatent_pb_t_kernel(tc, edge_hid, u, enc, W2, b2, W3, b3, out):
                         stop=(b == GRIDS - 1 and chain == CHAINS - 1),
                     )
 
-        regroup(nc, w2_grouped[:], w2_planes[:])
-        transpose_edge(0)
-        quantise(nc, w2_codes[:], w2_scales[:], w2_grouped[:])
-        quantise_edge(0)
+        def regroup_w3(part):
+            cols = slice(part * W3_PART, (part + 1) * W3_PART)
+            regroup(nc, w3_grouped[:, part * W3_PART * PACK : (part + 1) * W3_PART * PACK], w3_planes[:, :, cols])
+
+        def quantise_w3(part):
+            cols = slice(part * W3_PART, (part + 1) * W3_PART)
+            quantise(
+                nc,
+                w3_codes[:, cols],
+                w3_scales[:, cols],
+                w3_grouped[:, part * W3_PART * PACK : (part + 1) * W3_PART * PACK],
+            )
 
         vec_ps = psum_tp.tile([P, P], BF16, tag="tp")
         nc.tensor.transpose(vec_ps[:], vec_rows[:], ident_bf[:])
+        regroup(nc, w2_grouped[:], w2_planes[:])
         vec_cols = const.tile([P, VEC_ROWS], F32)
         nc.vector.tensor_copy(out=vec_cols[:], in_=vec_ps[:, 0:VEC_ROWS])
         enc_cols = vec_cols[:, ENC_ROW:VEC_ROWS]
         enc_sq = const.tile([P, LATENT_TILES], F32)
         nc.vector.tensor_tensor(out=enc_sq[:], in0=enc_cols, in1=enc_cols, op=ALU.mult)
-        s_ps = psum_tp.tile([P, LATENT_TILES], F32, tag="tp")
+        quantise(nc, w2_codes[:], w2_scales[:], w2_grouped[:])
+        transpose_edge(0, vector_halves=0)
+        quantise_edge(0)
+        transpose_edge(1, vector_halves=1)
+        quantise_edge(1)
+
+        s_ps = psum_z.tile([P, LATENT_TILES], F32, tag="z")
         nc.tensor.matmul(out=s_ps[:], lhsT=ones[:], rhs=enc_sq[:], start=True, stop=True)
         s_sum = const.tile([P, 1], F32)
         nc.vector.reduce_sum(out=s_sum[:], in_=s_ps[:], axis=AXIS.X)
@@ -240,23 +259,23 @@ def tile_fluxgnn1dlatent_pb_t_kernel(tc, edge_hid, u, enc, W2, b2, W3, b3, out):
         for g in range(-1, N_GROUPS + 1):
             if g + 1 < N_GROUPS:
                 layer1(g + 1)
-            if g + 2 < N_GROUPS:
-                transpose_edge(g + 2)
-            if g == -1:
-                regroup(nc, w3_grouped[:], w3_planes[:])
+            if g + 1 < W3_PARTS:
+                regroup_w3(g + 1)
+            if 2 <= g + 2 < N_GROUPS:
+                transpose_edge(g + 2, vector_halves=1)
+            if g + 1 < W3_PARTS:
+                quantise_w3(g + 1)
             if g + 1 < N_GROUPS:
                 regroup_x(g + 1)
-            if g + 2 < N_GROUPS:
+            if 2 <= g + 2 < N_GROUPS:
                 quantise_edge(g + 2)
-            if g == -1:
-                quantise(nc, w3_codes[:], w3_scales[:], w3_grouped[:])
             for j in range(LATENT_TILES):
                 if j == CHAINS and g + 1 < N_GROUPS:
                     quantise_x(g + 1)
+                if j == Z_BANKS and g >= 1:
+                    reduce_partitions(g - 1)
                 if 0 <= g < N_GROUPS:
                     layer2_tile(g, j)
-            if g >= 1:
-                reduce_partitions(g - 1)
 
         left = const.tile([GRIDS, CELLS], F32)
         nc.vector.tensor_tensor(out=left[:], in0=u_term[:], in1=g_sum[0:GRIDS, 0:CELLS], op=ALU.add)

@@ -61,12 +61,12 @@ def tile_fluxgnn1dlatent_pb_t_kernel(tc, edge_hid, u, enc, W2, b2, W3, b3, out):
         stack.enter_context(tc.manual_schedule())
 
         vec_rows = const.tile([P, P], BF16)
-        nc.vector.memset(vec_rows[:], 0.0)
-        nc.scalar.dma_start(out=vec_rows[B2_ROW:B3_ROW, :], in_=b2.rearrange("(t p) -> t p", p=P))
-        nc.scalar.dma_start(out=vec_rows[B3_ROW:ENC_ROW, :], in_=b3.rearrange("(t p) -> t p", p=P))
-        nc.scalar.dma_start(out=vec_rows[ENC_ROW:VEC_ROWS, :], in_=enc.rearrange("(t p) -> t p", p=P))
+        nc.gpsimd.memset(vec_rows[:], 0.0)
+        nc.sync.dma_start(out=vec_rows[B2_ROW:B3_ROW, :], in_=b2.rearrange("(t p) -> t p", p=P))
+        nc.sync.dma_start(out=vec_rows[B3_ROW:ENC_ROW, :], in_=b3.rearrange("(t p) -> t p", p=P))
+        nc.sync.dma_start(out=vec_rows[ENC_ROW:VEC_ROWS, :], in_=enc.rearrange("(t p) -> t p", p=P))
         u_bf = const.tile([GRIDS, CELLS], BF16)
-        nc.scalar.dma_start(out=u_bf[:], in_=u)
+        nc.sync.dma_start(out=u_bf[:], in_=u)
 
         w2_planes = const.tile([P, PACK, HID], BF16)
         nc.sync.dma_start(

@@ -25,9 +25,14 @@ GRIDS_PER_GROUP = GROUP // FACES
 HID_TILES = HID // P
 LATENT_TILES = LATENT // P
 CHAINS = 2
+TANH_BUFS = 12
 Z_BANKS = 5
-W3_PARTS = 2
+HALF = GROUP // 2
+W2_PARTS = 2
+W2_PART = HID // W2_PARTS
+W3_PARTS = 4
 W3_PART = LATENT // W3_PARTS
+LAST = N_GROUPS - 1
 FLUX_WEIGHT = 0.125
 B2_ROW = 0
 B3_ROW = B2_ROW + HID_TILES
@@ -37,8 +42,8 @@ VEC_ROWS = ENC_ROW + LATENT_TILES
 FLOPS = 2 * GRIDS * FACES * HID * (HID + LATENT)
 
 
-def regroup(nc, grouped, planes):
-    nc.vector.tensor_copy(
+def regroup(copy, grouped, planes):
+    copy(
         out=grouped.rearrange("p (c i t) -> p c t i", i=4, t=PACK),
         in_=planes.rearrange("p t (c i) -> p c t i", i=4),
     )
@@ -54,7 +59,7 @@ def tile_fluxgnn1dlatent_pb_t_kernel(tc, edge_hid, u, enc, W2, b2, W3, b3, out):
         const = stack.enter_context(tc.tile_pool(name="const", bufs=1))
         edge_pool = stack.enter_context(tc.tile_pool(name="edge", bufs=N_GROUPS))
         stage = stack.enter_context(tc.tile_pool(name="stage", bufs=2))
-        tanh_pool = stack.enter_context(tc.tile_pool(name="tanh", bufs=LATENT_TILES))
+        tanh_pool = stack.enter_context(tc.tile_pool(name="tanh", bufs=TANH_BUFS))
         psum_tp = stack.enter_context(tc.psum_pool(name="psum_tp", bufs=2))
         psum_z = stack.enter_context(tc.psum_pool(name="psum_z", bufs=Z_BANKS))
         psum_g = stack.enter_context(tc.psum_pool(name="psum_g", bufs=1))
@@ -65,23 +70,35 @@ def tile_fluxgnn1dlatent_pb_t_kernel(tc, edge_hid, u, enc, W2, b2, W3, b3, out):
         nc.sync.dma_start(out=vec_rows[B2_ROW:B3_ROW, :], in_=b2.rearrange("(t p) -> t p", p=P))
         nc.sync.dma_start(out=vec_rows[B3_ROW:ENC_ROW, :], in_=b3.rearrange("(t p) -> t p", p=P))
         nc.sync.dma_start(out=vec_rows[ENC_ROW:VEC_ROWS, :], in_=enc.rearrange("(t p) -> t p", p=P))
-        u_bf = const.tile([GRIDS, CELLS], BF16)
-        nc.sync.dma_start(out=u_bf[:], in_=u)
+        edge_view = edge_hid.flatten_outer_dims().rearrange("(g s p) k -> g p s k", s=GROUP // P, p=P)
+        edge_tiles = []
+
+        def load_edge(g, parts):
+            edge_rows = edge_pool.tile([P, GROUP // P, HID], BF16, tag="edge")
+            edge_tiles.append(edge_rows)
+            step = GROUP // P // parts
+            return [
+                lambda s=s: nc.sync.dma_start(out=edge_rows[:, s : s + step, :], in_=edge_view[g][:, s : s + step, :])
+                for s in range(0, GROUP // P, step)
+            ]
 
         w2_planes = const.tile([P, PACK, HID], BF16)
+        w3_planes = const.tile([P, PACK, LATENT], BF16)
+        w3_view = W3.rearrange("(t p) c -> p t c", p=P)
+        first_half, second_half = load_edge(0, 2)
+        first_half()
         nc.sync.dma_start(
             out=w2_planes[:].rearrange("p (h e) c -> p h e c", e=2),
             in_=W2.rearrange("(h p e) c -> p h e c", h=2, e=2),
         )
-        edge_view = edge_hid.flatten_outer_dims().rearrange("(g s p) k -> g p s k", s=GROUP // P, p=P)
-        edge_tiles = []
-        w3_planes = const.tile([P, PACK, LATENT], BF16)
-        for g in range(N_GROUPS):
-            edge_rows = edge_pool.tile([P, (GROUP // P) * HID], BF16, tag="edge")
-            nc.sync.dma_start(out=edge_rows[:].rearrange("p (s k) -> p s k", k=HID), in_=edge_view[g])
-            edge_tiles.append(edge_rows)
-            if g == 1:
-                nc.sync.dma_start(out=w3_planes[:], in_=W3.rearrange("(t p) c -> p t c", p=P))
+        second_half()
+        load_edge(1, 1)[0]()
+        for c in range(0, LATENT, LATENT // 2):
+            nc.sync.dma_start(out=w3_planes[:, :, c : c + LATENT // 2], in_=w3_view[:, :, c : c + LATENT // 2])
+        u_bf = const.tile([GRIDS, CELLS], BF16)
+        nc.sync.dma_start(out=u_bf[:], in_=u)
+        for g in range(2, N_GROUPS):
+            load_edge(g, 1)[0]()
 
         ident_bf = const.tile([P, P], BF16)
         make_identity(nc, ident_bf[:])
@@ -102,93 +119,98 @@ def tile_fluxgnn1dlatent_pb_t_kernel(tc, edge_hid, u, enc, W2, b2, W3, b3, out):
         w3_codes = const.tile([P, LATENT], U32, align_bytes=64)
         w3_scales = const.tile([P, LATENT], U8, align_bytes=64)
 
-        edge_codes = {}
+        transposed = {}
         edge_grouped = {}
+        edge_codes = {}
         x_planes = {}
         x_grouped = {}
         x_codes = {}
         sums = {}
+        fluxes = {}
+        ALL = slice(0, GROUP)
+        HALVES = (slice(0, HALF), slice(HALF, GROUP))
 
-        def transpose_edge(g, vector_halves):
-            words = edge_tiles[g][:].bitcast(F32)
-            grouped = stage.tile([P, GROUP * PACK], BF16, tag="edge_grouped", align_bytes=64)
-            grouped_words = grouped[:].bitcast(F32).rearrange("p (r h) -> p r h", h=2)
-            for half in range(2):
-                tp = psum_tp.tile([P, 2, FACES], F32, tag="tp")
-                for s in range(2):
-                    for h in range(2):
-                        first = (2 * half + s) * (HID // 2) + h * P
-                        nc.tensor.transpose(
-                            tp[:, h, s * P : (s + 1) * P], words[:, first : first + P], ident_f32[:]
-                        )
-                dst = grouped_words[:, half * FACES : (half + 1) * FACES, :]
-                src = tp[:].rearrange("p h r -> p r h")
-                if half < vector_halves:
-                    nc.vector.tensor_copy(out=dst, in_=src)
-                else:
-                    nc.scalar.copy(out=dst, in_=src)
-            edge_grouped[g] = grouped
+        def packed(cols):
+            return slice(cols.start * PACK, cols.stop * PACK)
 
-        def quantise_edge(g):
-            codes = stage.tile([P, GROUP], U32, tag="edge_codes", align_bytes=64)
-            scales = stage.tile([P, GROUP], U8, tag="edge_scales", align_bytes=64)
-            quantise(nc, codes[:], scales[:], edge_grouped[g][:])
-            edge_codes[g] = (codes, scales)
+        def transpose_edge(g, half, pool, tag):
+            words = edge_tiles[g][:].rearrange("p s k -> p (s k)").bitcast(F32)
+            tp = pool.tile([P, 2, HALF], F32, tag=tag)
+            for s in range(2):
+                for h in range(2):
+                    first = (2 * half + s) * (HID // 2) + h * P
+                    nc.tensor.transpose(tp[:, h, s * P : (s + 1) * P], words[:, first : first + P], ident_f32[:])
+            transposed[(g, half)] = tp
 
-        def layer1(g):
+        def copy_edge(g, half, copy):
+            if half == 0:
+                grouped = stage.tile([P, GROUP * PACK], BF16, tag="edge_grouped", align_bytes=64)
+                edge_grouped[g] = grouped
+            grouped_words = edge_grouped[g][:].bitcast(F32).rearrange("p (r h) -> p r h", h=2)
+            copy(out=grouped_words[:, HALVES[half], :], in_=transposed[(g, half)][:].rearrange("p h r -> p r h"))
+
+        def quantise_edge(g, cols):
+            if cols.start == 0:
+                codes = stage.tile([P, GROUP], U32, tag="edge_codes", align_bytes=64)
+                scales = stage.tile([P, GROUP], U8, tag="edge_scales", align_bytes=64)
+                edge_codes[g] = (codes, scales)
             codes, scales = edge_codes[g]
-            planes = stage.tile([P, PACK, GROUP], BF16, tag="x_planes")
-            for t in range(HID_TILES):
-                cols = slice(t * P, (t + 1) * P)
-                z = psum_z.tile([P, GROUP], F32, tag="z")
-                nc.tensor.matmul_mx(
-                    out=z[:],
-                    lhsT=w2_codes[:, cols].bitcast(FP8X4),
-                    lhsT_scale=w2_scales[:, cols],
-                    rhs=codes[:].bitcast(FP8X4),
-                    rhs_scale=scales[:],
-                    start=True,
-                    stop=True,
-                )
-                nc.scalar.activation(
-                    out=planes[:, t, :], in_=z[:], func=ACT.Gelu, bias=vec_cols[:, B2_ROW + t : B2_ROW + t + 1]
-                )
-            x_planes[g] = planes
+            quantise(nc, codes[:, cols], scales[:, cols], edge_grouped[g][:, packed(cols)])
 
-        def regroup_x(g):
-            grouped = stage.tile([P, GROUP * PACK], BF16, tag="x_grouped", align_bytes=64)
-            regroup(nc, grouped[:], x_planes[g][:])
-            x_grouped[g] = grouped
-
-        def quantise_x(g):
-            codes = stage.tile([P, GROUP], U32, tag="x_codes", align_bytes=64)
-            scales = stage.tile([P, GROUP], U8, tag="x_scales", align_bytes=64)
-            quantise(nc, codes[:], scales[:], x_grouped[g][:])
-            x_codes[g] = (codes, scales)
-
-        def layer2_tile(g, j):
-            codes, scales = x_codes[g]
-            cols = slice(j * P, (j + 1) * P)
-            z = psum_z.tile([P, GROUP], F32, tag="z")
+        def multiply(weights, tile, moving, cols):
+            channels = slice(tile * P, (tile + 1) * P)
+            z = psum_z.tile([P, cols.stop - cols.start], F32, tag="z")
             nc.tensor.matmul_mx(
                 out=z[:],
-                lhsT=w3_codes[:, cols].bitcast(FP8X4),
-                lhsT_scale=w3_scales[:, cols],
-                rhs=codes[:].bitcast(FP8X4),
-                rhs_scale=scales[:],
+                lhsT=weights[0][:, channels].bitcast(FP8X4),
+                lhsT_scale=weights[1][:, channels],
+                rhs=moving[0][:, cols].bitcast(FP8X4),
+                rhs_scale=moving[1][:, cols],
                 start=True,
                 stop=True,
             )
-            flux = tanh_pool.tile([P, GROUP], F32, tag="flux")
+            return z
+
+        def layer1(g, tiles, cols):
+            if g not in x_planes:
+                planes = stage.tile([P, PACK, GROUP], BF16, tag="x_planes")
+                x_planes[g] = planes
+            for t in tiles:
+                z = multiply((w2_codes, w2_scales), t, edge_codes[g], cols)
+                nc.scalar.activation(
+                    out=x_planes[g][:, t, cols], in_=z[:], func=ACT.Gelu, bias=vec_cols[:, B2_ROW + t : B2_ROW + t + 1]
+                )
+
+        def regroup_x(g, cols):
+            if cols.start == 0:
+                grouped = stage.tile([P, GROUP * PACK], BF16, tag="x_grouped", align_bytes=64)
+                x_grouped[g] = grouped
+            regroup(nc.vector.tensor_copy, x_grouped[g][:, packed(cols)], x_planes[g][:, :, cols])
+
+        def quantise_x(g, cols):
+            if cols.start == 0:
+                codes = stage.tile([P, GROUP], U32, tag="x_codes", align_bytes=64)
+                scales = stage.tile([P, GROUP], U8, tag="x_scales", align_bytes=64)
+                x_codes[g] = (codes, scales)
+            codes, scales = x_codes[g]
+            quantise(nc, codes[:, cols], scales[:, cols], x_grouped[g][:, packed(cols)])
+
+        def layer2_tanh(g, j, cols):
+            z = multiply((w3_codes, w3_scales), j, x_codes[g], cols)
+            flux = tanh_pool.tile([P, cols.stop - cols.start], F32, tag="flux")
             nc.scalar.activation(
                 out=flux[:], in_=z[:], func=ACT.Tanh, bias=vec_cols[:, B3_ROW + j : B3_ROW + j + 1]
             )
+            fluxes[(g, j, cols.start)] = flux
+
+        def layer2_sum(g, j, cols):
+            flux = fluxes[(g, j, cols.start)]
             if j < CHAINS:
-                partial = stage.tile([P, GROUP], F32, tag="sum%d" % j)
+                partial = stage.tile([P, cols.stop - cols.start], F32, tag="sum%d" % j)
                 nc.vector.tensor_scalar_mul(out=partial[:], in0=flux[:], scalar1=weight[:, j : j + 1])
-                sums[(g, j)] = partial
+                sums[(g, j, cols.start)] = partial
             else:
-                partial = sums[(g, j % CHAINS)]
+                partial = sums[(g, j % CHAINS, cols.start)]
                 nc.vector.scalar_tensor_tensor(
                     out=partial[:],
                     in0=flux[:],
@@ -198,84 +220,147 @@ def tile_fluxgnn1dlatent_pb_t_kernel(tc, edge_hid, u, enc, W2, b2, W3, b3, out):
                     op1=ALU.add,
                 )
 
-        def reduce_partitions(g):
-            for chain in range(CHAINS):
-                for grid in range(GRIDS_PER_GROUP):
-                    b = g * GRIDS_PER_GROUP + grid
-                    nc.tensor.matmul(
-                        out=g_sum[:],
-                        lhsT=window[:, P - b : 2 * P - b],
-                        rhs=sums[(g, chain)][:, grid * FACES : (grid + 1) * FACES],
-                        start=(b == 0 and chain == 0),
-                        stop=(b == GRIDS - 1 and chain == CHAINS - 1),
-                    )
+        def reduce_grid(b, partial, start, stop):
+            nc.tensor.matmul(
+                out=g_sum[:], lhsT=window[:, P - b : 2 * P - b], rhs=partial, start=start, stop=stop
+            )
+
+        def reduce_group(g, quarter):
+            chain, grid = divmod(quarter, GRIDS_PER_GROUP)
+            reduce_grid(
+                g * GRIDS_PER_GROUP + grid,
+                sums[(g, chain, 0)][:, HALVES[grid]],
+                start=(g == 0 and quarter == 0),
+                stop=False,
+            )
+
+        def regroup_w(copy, grouped, planes, part, width):
+            cols = slice(part * width, (part + 1) * width)
+            regroup(copy, grouped[:, packed(cols)], planes[:, :, cols])
+
+        def quantise_w(codes, scales, grouped, part, width):
+            cols = slice(part * width, (part + 1) * width)
+            quantise(nc, codes[:, cols], scales[:, cols], grouped[:, packed(cols)])
+
+        def regroup_w2(part, copy):
+            regroup_w(copy, w2_grouped, w2_planes, part, W2_PART)
+
+        def quantise_w2(part):
+            quantise_w(w2_codes, w2_scales, w2_grouped, part, W2_PART)
 
         def regroup_w3(part):
-            cols = slice(part * W3_PART, (part + 1) * W3_PART)
-            regroup(nc, w3_grouped[:, part * W3_PART * PACK : (part + 1) * W3_PART * PACK], w3_planes[:, :, cols])
+            regroup_w(nc.vector.tensor_copy, w3_grouped, w3_planes, part, W3_PART)
 
         def quantise_w3(part):
-            cols = slice(part * W3_PART, (part + 1) * W3_PART)
-            quantise(
-                nc,
-                w3_codes[:, cols],
-                w3_scales[:, cols],
-                w3_grouped[:, part * W3_PART * PACK : (part + 1) * W3_PART * PACK],
-            )
+            quantise_w(w3_codes, w3_scales, w3_grouped, part, W3_PART)
+
+        on_vector = nc.vector.tensor_copy
+        on_scalar = nc.scalar.copy
 
         vec_ps = psum_tp.tile([P, P], BF16, tag="tp")
         nc.tensor.transpose(vec_ps[:], vec_rows[:], ident_bf[:])
-        regroup(nc, w2_grouped[:], w2_planes[:])
         vec_cols = const.tile([P, VEC_ROWS], F32)
         nc.vector.tensor_copy(out=vec_cols[:], in_=vec_ps[:, 0:VEC_ROWS])
         enc_cols = vec_cols[:, ENC_ROW:VEC_ROWS]
         enc_sq = const.tile([P, LATENT_TILES], F32)
         nc.vector.tensor_tensor(out=enc_sq[:], in0=enc_cols, in1=enc_cols, op=ALU.mult)
-        quantise(nc, w2_codes[:], w2_scales[:], w2_grouped[:])
-        transpose_edge(0, vector_halves=0)
-        quantise_edge(0)
-        transpose_edge(1, vector_halves=1)
-        quantise_edge(1)
+        s_sum = const.tile([P, 1], F32)
+        s_eps = const.tile([P, 1], F32)
+        s_inv = const.tile([P, 1], F32)
+        weight = const.tile([P, LATENT_TILES], F32)
+        u_gain = const.tile([P, 1], F32)
+        u_term = const.tile([GRIDS, CELLS], F32)
+        g_sum = psum_g.tile([P, FACES], F32)
 
+        transpose_edge(0, 0, psum_tp, "tp")
+        copy_edge(0, 0, on_scalar)
+        regroup_w2(0, on_vector)
+        regroup_w2(1, on_scalar)
+        transpose_edge(0, 1, psum_tp, "tp")
+        quantise_edge(0, HALVES[0])
+        quantise_w2(0)
         s_ps = psum_z.tile([P, LATENT_TILES], F32, tag="z")
         nc.tensor.matmul(out=s_ps[:], lhsT=ones[:], rhs=enc_sq[:], start=True, stop=True)
-        s_sum = const.tile([P, 1], F32)
         nc.vector.reduce_sum(out=s_sum[:], in_=s_ps[:], axis=AXIS.X)
-        s_eps = const.tile([P, 1], F32)
+        copy_edge(0, 1, on_scalar)
+        layer1(0, (0, 1), HALVES[0])
+        quantise_w2(1)
         nc.vector.tensor_scalar_add(out=s_eps[:], in0=s_sum[:], scalar1=1e-12)
-        s_inv = const.tile([P, 1], F32)
+        quantise_edge(0, HALVES[1])
         nc.vector.reciprocal(out=s_inv[:], in_=s_eps[:])
-        weight = const.tile([P, LATENT_TILES], F32)
+        layer1(0, (2, 3), HALVES[0])
+        transpose_edge(1, 0, psum_z, "z")
+        copy_edge(1, 0, on_scalar)
+        transpose_edge(1, 1, psum_tp, "tp")
+        regroup_w3(0)
+        regroup_w3(1)
+        layer1(0, range(HID_TILES), HALVES[1])
+        copy_edge(1, 1, on_vector)
+        quantise_w3(0)
+        quantise_edge(1, ALL)
+        transpose_edge(2, 0, psum_tp, "tp")
+        copy_edge(2, 0, on_scalar)
+        regroup_x(0, HALVES[0])
+        layer1(1, range(HID_TILES), ALL)
+        regroup_x(0, HALVES[1])
+        quantise_x(0, HALVES[0])
         nc.vector.tensor_scalar(
             out=weight[:], in0=enc_cols, scalar1=s_inv[:, 0:1], scalar2=FLUX_WEIGHT, op0=ALU.mult, op1=ALU.mult
         )
-        u_gain = const.tile([P, 1], F32)
         nc.vector.tensor_tensor(out=u_gain[:], in0=s_sum[:], in1=s_inv[:], op=ALU.mult)
-        u_term = const.tile([GRIDS, CELLS], F32)
+        quantise_x(0, HALVES[1])
+        for j in range(2):
+            layer2_tanh(0, j, ALL)
+        transpose_edge(2, 1, psum_tp, "tp")
+        copy_edge(2, 1, on_scalar)
+        regroup_w3(2)
+        quantise_w3(1)
+        quantise_w3(2)
+        for j in range(2, 6):
+            layer2_tanh(0, j, ALL)
+        regroup_w3(3)
+        layer2_sum(0, 0, ALL)
+        quantise_w3(3)
+        layer2_sum(0, 1, ALL)
+        for j in range(6, LATENT_TILES):
+            layer2_tanh(0, j, ALL)
+        quantise_edge(2, ALL)
+        regroup_x(1, ALL)
+        layer2_sum(0, 2, ALL)
+        quantise_x(1, ALL)
+        for j in range(3, LATENT_TILES):
+            layer2_sum(0, j, ALL)
         nc.vector.tensor_scalar_mul(out=u_term[:], in0=u_bf[:], scalar1=u_gain[0:GRIDS, 0:1])
 
-        g_sum = psum_g.tile([P, FACES], F32)
-
-        for g in range(-1, N_GROUPS + 1):
-            if g + 1 < N_GROUPS:
-                layer1(g + 1)
-            if g + 1 < W3_PARTS:
-                regroup_w3(g + 1)
-            if 2 <= g + 2 < N_GROUPS:
-                transpose_edge(g + 2, vector_halves=1)
-            if g + 1 < W3_PARTS:
-                quantise_w3(g + 1)
-            if g + 1 < N_GROUPS:
-                regroup_x(g + 1)
-            if 2 <= g + 2 < N_GROUPS:
-                quantise_edge(g + 2)
+        for g in range(1, LAST):
+            layer1(g + 1, range(HID_TILES), ALL)
+            if g + 2 < N_GROUPS:
+                for half, copy in enumerate((on_vector, on_scalar)):
+                    transpose_edge(g + 2, half, psum_tp, "tp")
+                    copy_edge(g + 2, half, copy)
+            regroup_x(g + 1, ALL)
+            if g + 2 < N_GROUPS:
+                quantise_edge(g + 2, ALL)
             for j in range(LATENT_TILES):
-                if j == CHAINS and g + 1 < N_GROUPS:
-                    quantise_x(g + 1)
-                if j == Z_BANKS and g >= 1:
-                    reduce_partitions(g - 1)
-                if 0 <= g < N_GROUPS:
-                    layer2_tile(g, j)
+                if j == CHAINS:
+                    quantise_x(g + 1, ALL)
+                layer2_tanh(g, j, ALL)
+                layer2_sum(g, j, ALL)
+                if 3 <= j < 7:
+                    reduce_group(g - 1, j - 3)
+
+        last_grids = (GRIDS - 2, GRIDS - 1)
+        for half, cols in enumerate(HALVES):
+            for j in range(LATENT_TILES):
+                layer2_tanh(LAST, j, cols)
+                layer2_sum(LAST, j, cols)
+                if half == 1 and 3 <= j < 7:
+                    reduce_group(LAST - 1, j - 3)
+        for cols, b in zip(HALVES, last_grids):
+            for chain in range(CHAINS):
+                reduce_grid(
+                    b, sums[(LAST, chain, cols.start)][:], start=False, stop=(b == GRIDS - 1 and chain == CHAINS - 1)
+                )
 
         left = const.tile([GRIDS, CELLS], F32)
         nc.vector.tensor_tensor(out=left[:], in0=u_term[:], in1=g_sum[0:GRIDS, 0:CELLS], op=ALU.add)

@@ -33,6 +33,7 @@ W2_PART = HID // W2_PARTS
 W3_PARTS = 4
 W3_PART = LATENT // W3_PARTS
 LAST = N_GROUPS - 1
+CELLS_PER_GROUP = GRIDS_PER_GROUP * CELLS
 FLUX_WEIGHT = 0.125
 B2_ROW = 0
 B3_ROW = B2_ROW + HID_TILES
@@ -95,8 +96,10 @@ def tile_fluxgnn1dlatent_pb_t_kernel(tc, edge_hid, u, enc, W2, b2, W3, b3, out):
         load_edge(1, 1)[0]()
         for c in range(0, LATENT, LATENT // 2):
             nc.sync.dma_start(out=w3_planes[:, :, c : c + LATENT // 2], in_=w3_view[:, :, c : c + LATENT // 2])
-        u_bf = const.tile([GRIDS, CELLS], BF16)
-        nc.sync.dma_start(out=u_bf[:], in_=u)
+        u_bf = const.tile([N_GROUPS, CELLS_PER_GROUP], BF16)
+        nc.sync.dma_start(out=u_bf[:], in_=u.rearrange("(g r) c -> g (r c)", r=GRIDS_PER_GROUP))
+        u_last = const.tile([GRIDS_PER_GROUP, CELLS], BF16)
+        nc.sync.dma_start(out=u_last[:], in_=u[GRIDS - GRIDS_PER_GROUP : GRIDS, :])
         for g in range(2, N_GROUPS):
             load_edge(g, 1)[0]()
 
@@ -220,18 +223,18 @@ def tile_fluxgnn1dlatent_pb_t_kernel(tc, edge_hid, u, enc, W2, b2, W3, b3, out):
                     op1=ALU.add,
                 )
 
-        def reduce_grid(b, partial, start, stop):
+        def reduce_partitions(out_tile, row, partial, start, stop):
             nc.tensor.matmul(
-                out=g_sum[:], lhsT=window[:, P - b : 2 * P - b], rhs=partial, start=start, stop=stop
+                out=out_tile[:], lhsT=window[:, P - row : 2 * P - row], rhs=partial[:], start=start, stop=stop
             )
 
-        def reduce_group(g, quarter):
-            chain, grid = divmod(quarter, GRIDS_PER_GROUP)
-            reduce_grid(
-                g * GRIDS_PER_GROUP + grid,
-                sums[(g, chain, 0)][:, HALVES[grid]],
-                start=(g == 0 and quarter == 0),
-                stop=False,
+        def reduce_group(g, chain):
+            reduce_partitions(
+                g_sum,
+                g,
+                sums[(g, chain, 0)],
+                start=(g == 0 and chain == 0),
+                stop=(g == LAST - 1 and chain == CHAINS - 1),
             )
 
         def regroup_w(copy, grouped, planes, part, width):
@@ -269,8 +272,9 @@ def tile_fluxgnn1dlatent_pb_t_kernel(tc, edge_hid, u, enc, W2, b2, W3, b3, out):
         s_inv = const.tile([P, 1], F32)
         weight = const.tile([P, LATENT_TILES], F32)
         u_gain = const.tile([P, 1], F32)
-        u_term = const.tile([GRIDS, CELLS], F32)
-        g_sum = psum_g.tile([P, FACES], F32)
+        u_term = const.tile([N_GROUPS, CELLS_PER_GROUP], F32)
+        u_last_term = const.tile([GRIDS_PER_GROUP, CELLS], F32)
+        g_sum = psum_g.tile([P, GROUP], F32)
 
         transpose_edge(0, 0, psum_tp, "tp")
         copy_edge(0, 0, on_scalar)
@@ -330,7 +334,8 @@ def tile_fluxgnn1dlatent_pb_t_kernel(tc, edge_hid, u, enc, W2, b2, W3, b3, out):
         quantise_x(1, ALL)
         for j in range(3, LATENT_TILES):
             layer2_sum(0, j, ALL)
-        nc.vector.tensor_scalar_mul(out=u_term[:], in0=u_bf[:], scalar1=u_gain[0:GRIDS, 0:1])
+        nc.vector.tensor_scalar_mul(out=u_term[:], in0=u_bf[:], scalar1=u_gain[0:N_GROUPS, 0:1])
+        nc.vector.tensor_scalar_mul(out=u_last_term[:], in0=u_last[:], scalar1=u_gain[0:GRIDS_PER_GROUP, 0:1])
 
         for g in range(1, LAST):
             layer1(g + 1, range(HID_TILES), ALL)
@@ -346,24 +351,50 @@ def tile_fluxgnn1dlatent_pb_t_kernel(tc, edge_hid, u, enc, W2, b2, W3, b3, out):
                     quantise_x(g + 1, ALL)
                 layer2_tanh(g, j, ALL)
                 layer2_sum(g, j, ALL)
-                if 3 <= j < 7:
-                    reduce_group(g - 1, j - 3)
+                if j in (3, 5):
+                    reduce_group(g - 1, j // 2 - 1)
 
-        last_grids = (GRIDS - 2, GRIDS - 1)
+        g_last = psum_tp.tile([P, FACES], F32, tag="tp")
         for half, cols in enumerate(HALVES):
             for j in range(LATENT_TILES):
                 layer2_tanh(LAST, j, cols)
                 layer2_sum(LAST, j, cols)
-                if half == 1 and 3 <= j < 7:
-                    reduce_group(LAST - 1, j - 3)
-        for cols, b in zip(HALVES, last_grids):
+                if half == 1 and j in (3, 5):
+                    reduce_group(LAST - 1, j // 2 - 1)
+        for grid, cols in enumerate(HALVES):
             for chain in range(CHAINS):
-                reduce_grid(
-                    b, sums[(LAST, chain, cols.start)][:], start=False, stop=(b == GRIDS - 1 and chain == CHAINS - 1)
+                reduce_partitions(
+                    g_last,
+                    grid,
+                    sums[(LAST, chain, cols.start)],
+                    start=(grid == 0 and chain == 0),
+                    stop=(grid == GRIDS_PER_GROUP - 1 and chain == CHAINS - 1),
                 )
 
-        left = const.tile([GRIDS, CELLS], F32)
-        nc.vector.tensor_tensor(out=left[:], in0=u_term[:], in1=g_sum[0:GRIDS, 0:CELLS], op=ALU.add)
-        result = const.tile([GRIDS, CELLS], F32)
-        nc.vector.tensor_tensor(out=result[:], in0=left[:], in1=g_sum[0:GRIDS, 1:FACES], op=ALU.subtract)
-        nc.sync.dma_start(out=out, in_=result[:])
+        faces = g_sum[0:LAST, :].rearrange("g (r f) -> g r f", f=FACES)
+        left = const.tile([LAST, CELLS_PER_GROUP], F32)
+        nc.vector.tensor_tensor(
+            out=left[:].rearrange("g (r c) -> g r c", c=CELLS),
+            in0=u_term[0:LAST, :].rearrange("g (r c) -> g r c", c=CELLS),
+            in1=faces[:, :, 0:CELLS],
+            op=ALU.add,
+        )
+        result = const.tile([LAST, CELLS_PER_GROUP], F32)
+        nc.vector.tensor_tensor(
+            out=result[:].rearrange("g (r c) -> g r c", c=CELLS),
+            in0=left[:].rearrange("g (r c) -> g r c", c=CELLS),
+            in1=faces[:, :, 1:FACES],
+            op=ALU.subtract,
+        )
+        nc.sync.dma_start(
+            out=out[0 : LAST * GRIDS_PER_GROUP, :].rearrange("(g r) c -> g (r c)", r=GRIDS_PER_GROUP), in_=result[:]
+        )
+        left_last = const.tile([GRIDS_PER_GROUP, CELLS], F32)
+        nc.vector.tensor_tensor(
+            out=left_last[:], in0=u_last_term[:], in1=g_last[0:GRIDS_PER_GROUP, 0:CELLS], op=ALU.add
+        )
+        result_last = const.tile([GRIDS_PER_GROUP, CELLS], F32)
+        nc.vector.tensor_tensor(
+            out=result_last[:], in0=left_last[:], in1=g_last[0:GRIDS_PER_GROUP, 1:FACES], op=ALU.subtract
+        )
+        nc.sync.dma_start(out=out[GRIDS - GRIDS_PER_GROUP : GRIDS, :], in_=result_last[:])

@@ -27,6 +27,8 @@ LATENT_TILES = LATENT // P
 CHAINS = 2
 TANH_BUFS = 12
 Z_BANKS = 5
+ROWS = FACES // P
+BOTH = slice(0, GRIDS_PER_GROUP)
 HALF = GROUP // 2
 W2_PARTS = 2
 W2_PART = HID // W2_PARTS
@@ -68,32 +70,31 @@ def tile_fluxgnn1dlatent_pb_t_kernel(tc, edge_hid, u, enc, W2, b2, W3, b3, out):
 
         vec_rows = const.tile([P, P], BF16)
         nc.gpsimd.memset(vec_rows[:], 0.0)
-        nc.sync.dma_start(out=vec_rows[B2_ROW:B3_ROW, :], in_=b2.rearrange("(t p) -> t p", p=P))
-        nc.sync.dma_start(out=vec_rows[B3_ROW:ENC_ROW, :], in_=b3.rearrange("(t p) -> t p", p=P))
-        nc.sync.dma_start(out=vec_rows[ENC_ROW:VEC_ROWS, :], in_=enc.rearrange("(t p) -> t p", p=P))
-        edge_view = edge_hid.flatten_outer_dims().rearrange("(g s p) k -> g p s k", s=GROUP // P, p=P)
+        edge_view = edge_hid.rearrange("b (p s) k -> p b (s k)", s=ROWS)
         edge_tiles = []
-
-        def load_edge(g, parts):
-            edge_rows = edge_pool.tile([P, GROUP // P, HID], BF16, tag="edge")
+        for g in range(N_GROUPS):
+            edge_rows = edge_pool.tile([P, GRIDS_PER_GROUP, ROWS * HID], BF16, tag="edge")
             edge_tiles.append(edge_rows)
-            step = GROUP // P // parts
-            return [
-                lambda s=s: nc.sync.dma_start(out=edge_rows[:, s : s + step, :], in_=edge_view[g][:, s : s + step, :])
-                for s in range(0, GROUP // P, step)
-            ]
+
+        def load_edge(g, grids):
+            first = g * GRIDS_PER_GROUP
+            nc.sync.dma_start(
+                out=edge_tiles[g][:, grids, :], in_=edge_view[:, first + grids.start : first + grids.stop, :]
+            )
 
         w2_planes = const.tile([P, PACK, HID], BF16)
         w3_planes = const.tile([P, PACK, LATENT], BF16)
         w3_view = W3.rearrange("(t p) c -> p t c", p=P)
-        first_half, second_half = load_edge(0, 2)
-        first_half()
+        load_edge(0, slice(0, 1))
         nc.sync.dma_start(
             out=w2_planes[:].rearrange("p (h e) c -> p h e c", e=2),
             in_=W2.rearrange("(h p e) c -> p h e c", h=2, e=2),
         )
-        second_half()
-        load_edge(1, 1)[0]()
+        nc.sync.dma_start(out=vec_rows[B2_ROW:B3_ROW, :], in_=b2.rearrange("(t p) -> t p", p=P))
+        nc.sync.dma_start(out=vec_rows[B3_ROW:ENC_ROW, :], in_=b3.rearrange("(t p) -> t p", p=P))
+        nc.sync.dma_start(out=vec_rows[ENC_ROW:VEC_ROWS, :], in_=enc.rearrange("(t p) -> t p", p=P))
+        load_edge(0, slice(1, 2))
+        load_edge(1, BOTH)
         for c in range(0, LATENT, LATENT // 2):
             nc.sync.dma_start(out=w3_planes[:, :, c : c + LATENT // 2], in_=w3_view[:, :, c : c + LATENT // 2])
         u_bf = const.tile([N_GROUPS, CELLS_PER_GROUP], BF16)
@@ -101,7 +102,7 @@ def tile_fluxgnn1dlatent_pb_t_kernel(tc, edge_hid, u, enc, W2, b2, W3, b3, out):
         u_last = const.tile([GRIDS_PER_GROUP, CELLS], BF16)
         nc.sync.dma_start(out=u_last[:], in_=u[GRIDS - GRIDS_PER_GROUP : GRIDS, :])
         for g in range(2, N_GROUPS):
-            load_edge(g, 1)[0]()
+            load_edge(g, BOTH)
 
         ident_bf = const.tile([P, P], BF16)
         make_identity(nc, ident_bf[:])
@@ -137,11 +138,11 @@ def tile_fluxgnn1dlatent_pb_t_kernel(tc, edge_hid, u, enc, W2, b2, W3, b3, out):
             return slice(cols.start * PACK, cols.stop * PACK)
 
         def transpose_edge(g, half, pool, tag):
-            words = edge_tiles[g][:].rearrange("p s k -> p (s k)").bitcast(F32)
+            words = edge_tiles[g][:, half, :].bitcast(F32)
             tp = pool.tile([P, 2, HALF], F32, tag=tag)
-            for s in range(2):
+            for s in range(ROWS):
                 for h in range(2):
-                    first = (2 * half + s) * (HID // 2) + h * P
+                    first = s * (HID // 2) + h * P
                     nc.tensor.transpose(tp[:, h, s * P : (s + 1) * P], words[:, first : first + P], ident_f32[:])
             transposed[(g, half)] = tp
 
@@ -149,8 +150,11 @@ def tile_fluxgnn1dlatent_pb_t_kernel(tc, edge_hid, u, enc, W2, b2, W3, b3, out):
             if half == 0:
                 grouped = stage.tile([P, GROUP * PACK], BF16, tag="edge_grouped", align_bytes=64)
                 edge_grouped[g] = grouped
-            grouped_words = edge_grouped[g][:].bitcast(F32).rearrange("p (r h) -> p r h", h=2)
-            copy(out=grouped_words[:, HALVES[half], :], in_=transposed[(g, half)][:].rearrange("p h r -> p r h"))
+            grouped_words = edge_grouped[g][:, packed(HALVES[half])].bitcast(F32)
+            copy(
+                out=grouped_words.rearrange("p (r s h) -> p r s h", s=ROWS, h=2),
+                in_=transposed[(g, half)][:].rearrange("p h (s r) -> p r s h", s=ROWS),
+            )
 
         def quantise_edge(g, cols):
             if cols.start == 0:
@@ -260,13 +264,9 @@ def tile_fluxgnn1dlatent_pb_t_kernel(tc, edge_hid, u, enc, W2, b2, W3, b3, out):
         on_vector = nc.vector.tensor_copy
         on_scalar = nc.scalar.copy
 
-        vec_ps = psum_tp.tile([P, P], BF16, tag="tp")
-        nc.tensor.transpose(vec_ps[:], vec_rows[:], ident_bf[:])
         vec_cols = const.tile([P, VEC_ROWS], F32)
-        nc.vector.tensor_copy(out=vec_cols[:], in_=vec_ps[:, 0:VEC_ROWS])
         enc_cols = vec_cols[:, ENC_ROW:VEC_ROWS]
         enc_sq = const.tile([P, LATENT_TILES], F32)
-        nc.vector.tensor_tensor(out=enc_sq[:], in0=enc_cols, in1=enc_cols, op=ALU.mult)
         s_sum = const.tile([P, 1], F32)
         s_eps = const.tile([P, 1], F32)
         s_inv = const.tile([P, 1], F32)
@@ -280,8 +280,12 @@ def tile_fluxgnn1dlatent_pb_t_kernel(tc, edge_hid, u, enc, W2, b2, W3, b3, out):
         copy_edge(0, 0, on_scalar)
         regroup_w2(0, on_vector)
         regroup_w2(1, on_scalar)
+        vec_ps = psum_z.tile([P, P], BF16, tag="z")
+        nc.tensor.transpose(vec_ps[:], vec_rows[:], ident_bf[:])
         transpose_edge(0, 1, psum_tp, "tp")
+        nc.vector.tensor_copy(out=vec_cols[:], in_=vec_ps[:, 0:VEC_ROWS])
         quantise_edge(0, HALVES[0])
+        nc.vector.tensor_tensor(out=enc_sq[:], in0=enc_cols, in1=enc_cols, op=ALU.mult)
         quantise_w2(0)
         s_ps = psum_z.tile([P, LATENT_TILES], F32, tag="z")
         nc.tensor.matmul(out=s_ps[:], lhsT=ones[:], rhs=enc_sq[:], start=True, stop=True)

@@ -97,12 +97,14 @@ def tile_fluxgnn1dlatent_pb_t_kernel(tc, edge_hid, u, enc, W2, b2, W3, b3, out):
         load_edge(1, BOTH)
         for c in range(0, LATENT, LATENT // 2):
             nc.sync.dma_start(out=w3_planes[:, :, c : c + LATENT // 2], in_=w3_view[:, :, c : c + LATENT // 2])
+            if c == 0:
+                load_edge(2, BOTH)
+        for g in range(3, N_GROUPS):
+            load_edge(g, BOTH)
         u_bf = const.tile([N_GROUPS, CELLS_PER_GROUP], BF16)
         nc.sync.dma_start(out=u_bf[:], in_=u.rearrange("(g r) c -> g (r c)", r=GRIDS_PER_GROUP))
         u_last = const.tile([GRIDS_PER_GROUP, CELLS], BF16)
         nc.sync.dma_start(out=u_last[:], in_=u[GRIDS - GRIDS_PER_GROUP : GRIDS, :])
-        for g in range(2, N_GROUPS):
-            load_edge(g, BOTH)
 
         ident_bf = const.tile([P, P], BF16)
         make_identity(nc, ident_bf[:])
@@ -202,22 +204,22 @@ def tile_fluxgnn1dlatent_pb_t_kernel(tc, edge_hid, u, enc, W2, b2, W3, b3, out):
             codes, scales = x_codes[g]
             quantise(nc, codes[:, cols], scales[:, cols], x_grouped[g][:, packed(cols)])
 
-        def layer2_tanh(g, j, cols):
-            z = multiply((w3_codes, w3_scales), j, x_codes[g], cols)
-            flux = tanh_pool.tile([P, cols.stop - cols.start], F32, tag="flux")
+        def layer2_tanh(g, j):
+            z = multiply((w3_codes, w3_scales), j, x_codes[g], ALL)
+            flux = tanh_pool.tile([P, GROUP], F32, tag="flux")
             nc.scalar.activation(
                 out=flux[:], in_=z[:], func=ACT.Tanh, bias=vec_cols[:, B3_ROW + j : B3_ROW + j + 1]
             )
-            fluxes[(g, j, cols.start)] = flux
+            fluxes[(g, j)] = flux
 
-        def layer2_sum(g, j, cols):
-            flux = fluxes[(g, j, cols.start)]
+        def layer2_sum(g, j):
+            flux = fluxes[(g, j)]
             if j < CHAINS:
-                partial = stage.tile([P, cols.stop - cols.start], F32, tag="sum%d" % j)
+                partial = stage.tile([P, GROUP], F32, tag="sum%d" % j)
                 nc.vector.tensor_scalar_mul(out=partial[:], in0=flux[:], scalar1=weight[:, j : j + 1])
-                sums[(g, j, cols.start)] = partial
+                sums[(g, j)] = partial
             else:
-                partial = sums[(g, j % CHAINS, cols.start)]
+                partial = sums[(g, j % CHAINS)]
                 nc.vector.scalar_tensor_tensor(
                     out=partial[:],
                     in0=flux[:],
@@ -229,14 +231,14 @@ def tile_fluxgnn1dlatent_pb_t_kernel(tc, edge_hid, u, enc, W2, b2, W3, b3, out):
 
         def reduce_partitions(out_tile, row, partial, start, stop):
             nc.tensor.matmul(
-                out=out_tile[:], lhsT=window[:, P - row : 2 * P - row], rhs=partial[:], start=start, stop=stop
+                out=out_tile[:], lhsT=window[:, P - row : 2 * P - row], rhs=partial, start=start, stop=stop
             )
 
         def reduce_group(g, chain):
             reduce_partitions(
                 g_sum,
                 g,
-                sums[(g, chain, 0)],
+                sums[(g, chain)][:],
                 start=(g == 0 and chain == 0),
                 stop=(g == LAST - 1 and chain == CHAINS - 1),
             )
@@ -318,28 +320,26 @@ def tile_fluxgnn1dlatent_pb_t_kernel(tc, edge_hid, u, enc, W2, b2, W3, b3, out):
         nc.vector.tensor_tensor(out=u_gain[:], in0=s_sum[:], in1=s_inv[:], op=ALU.mult)
         quantise_x(0, HALVES[1])
         for j in range(2):
-            layer2_tanh(0, j, ALL)
+            layer2_tanh(0, j)
         transpose_edge(2, 1, psum_tp, "tp")
         copy_edge(2, 1, on_scalar)
         regroup_w3(2)
         quantise_w3(1)
         quantise_w3(2)
         for j in range(2, 6):
-            layer2_tanh(0, j, ALL)
+            layer2_tanh(0, j)
         regroup_w3(3)
-        layer2_sum(0, 0, ALL)
+        layer2_sum(0, 0)
         quantise_w3(3)
-        layer2_sum(0, 1, ALL)
+        layer2_sum(0, 1)
         for j in range(6, LATENT_TILES):
-            layer2_tanh(0, j, ALL)
+            layer2_tanh(0, j)
         quantise_edge(2, ALL)
         regroup_x(1, ALL)
-        layer2_sum(0, 2, ALL)
+        layer2_sum(0, 2)
         quantise_x(1, ALL)
         for j in range(3, LATENT_TILES):
-            layer2_sum(0, j, ALL)
-        nc.vector.tensor_scalar_mul(out=u_term[:], in0=u_bf[:], scalar1=u_gain[0:N_GROUPS, 0:1])
-        nc.vector.tensor_scalar_mul(out=u_last_term[:], in0=u_last[:], scalar1=u_gain[0:GRIDS_PER_GROUP, 0:1])
+            layer2_sum(0, j)
 
         for g in range(1, LAST):
             layer1(g + 1, range(HID_TILES), ALL)
@@ -353,27 +353,28 @@ def tile_fluxgnn1dlatent_pb_t_kernel(tc, edge_hid, u, enc, W2, b2, W3, b3, out):
             for j in range(LATENT_TILES):
                 if j == CHAINS:
                     quantise_x(g + 1, ALL)
-                layer2_tanh(g, j, ALL)
-                layer2_sum(g, j, ALL)
+                layer2_tanh(g, j)
+                layer2_sum(g, j)
                 if j in (3, 5):
                     reduce_group(g - 1, j // 2 - 1)
 
+        for j in range(LATENT_TILES):
+            layer2_tanh(LAST, j)
+            layer2_sum(LAST, j)
+        for chain in range(CHAINS):
+            reduce_group(LAST - 1, chain)
         g_last = psum_tp.tile([P, FACES], F32, tag="tp")
-        for half, cols in enumerate(HALVES):
-            for j in range(LATENT_TILES):
-                layer2_tanh(LAST, j, cols)
-                layer2_sum(LAST, j, cols)
-                if half == 1 and j in (3, 5):
-                    reduce_group(LAST - 1, j // 2 - 1)
-        for grid, cols in enumerate(HALVES):
-            for chain in range(CHAINS):
+        for chain in range(CHAINS):
+            for grid, cols in enumerate(HALVES):
                 reduce_partitions(
                     g_last,
                     grid,
-                    sums[(LAST, chain, cols.start)],
-                    start=(grid == 0 and chain == 0),
-                    stop=(grid == GRIDS_PER_GROUP - 1 and chain == CHAINS - 1),
+                    sums[(LAST, chain)][:, cols],
+                    start=(chain == 0 and grid == 0),
+                    stop=(chain == CHAINS - 1 and grid == GRIDS_PER_GROUP - 1),
                 )
+        nc.vector.tensor_scalar_mul(out=u_term[:], in0=u_bf[:], scalar1=u_gain[0:N_GROUPS, 0:1])
+        nc.vector.tensor_scalar_mul(out=u_last_term[:], in0=u_last[:], scalar1=u_gain[0:GRIDS_PER_GROUP, 0:1])
 
         faces = g_sum[0:LAST, :].rearrange("g (r f) -> g r f", f=FACES)
         left = const.tile([LAST, CELLS_PER_GROUP], F32)

@@ -35,7 +35,6 @@ W2_PART = HID // W2_PARTS
 W3_PARTS = 4
 W3_PART = LATENT // W3_PARTS
 LAST = N_GROUPS - 1
-CELLS_PER_GROUP = GRIDS_PER_GROUP * CELLS
 FLUX_WEIGHT = 0.125
 B2_ROW = 0
 B3_ROW = B2_ROW + HID_TILES
@@ -101,10 +100,8 @@ def tile_fluxgnn1dlatent_pb_t_kernel(tc, edge_hid, u, enc, W2, b2, W3, b3, out):
                 load_edge(2, BOTH)
         for g in range(3, N_GROUPS):
             load_edge(g, BOTH)
-        u_bf = const.tile([N_GROUPS, CELLS_PER_GROUP], BF16)
-        nc.sync.dma_start(out=u_bf[:], in_=u.rearrange("(g r) c -> g (r c)", r=GRIDS_PER_GROUP))
-        u_last = const.tile([GRIDS_PER_GROUP, CELLS], BF16)
-        nc.sync.dma_start(out=u_last[:], in_=u[GRIDS - GRIDS_PER_GROUP : GRIDS, :])
+        u_bf = const.tile([GRIDS, CELLS], BF16)
+        nc.sync.dma_start(out=u_bf[:], in_=u)
 
         ident_bf = const.tile([P, P], BF16)
         make_identity(nc, ident_bf[:])
@@ -219,7 +216,7 @@ def tile_fluxgnn1dlatent_pb_t_kernel(tc, edge_hid, u, enc, W2, b2, W3, b3, out):
                 nc.vector.tensor_scalar_mul(out=partial[:], in0=flux[:], scalar1=weight[:, j : j + 1])
                 sums[(g, j)] = partial
             else:
-                partial = sums[(g, j % CHAINS)]
+                partial = sums[(g, (j - 1 if (g, j) == (LAST, LATENT_TILES - 1) else j) % CHAINS)]
                 nc.vector.scalar_tensor_tensor(
                     out=partial[:],
                     in0=flux[:],
@@ -229,19 +226,16 @@ def tile_fluxgnn1dlatent_pb_t_kernel(tc, edge_hid, u, enc, W2, b2, W3, b3, out):
                     op1=ALU.add,
                 )
 
-        def reduce_partitions(out_tile, row, partial, start, stop):
-            nc.tensor.matmul(
-                out=out_tile[:], lhsT=window[:, P - row : 2 * P - row], rhs=partial, start=start, stop=stop
-            )
-
         def reduce_group(g, chain):
-            reduce_partitions(
-                g_sum,
-                g,
-                sums[(g, chain)][:],
-                start=(g == 0 and chain == 0),
-                stop=(g == LAST - 1 and chain == CHAINS - 1),
-            )
+            for grid, cols in enumerate(HALVES):
+                b = g * GRIDS_PER_GROUP + grid
+                nc.tensor.matmul(
+                    out=g_sum[:],
+                    lhsT=window[:, P - b : 2 * P - b],
+                    rhs=sums[(g, chain)][:, cols],
+                    start=(b == 0 and chain == 0),
+                    stop=(b == GRIDS - 1 and chain == 0),
+                )
 
         def regroup_w(copy, grouped, planes, part, width):
             cols = slice(part * width, (part + 1) * width)
@@ -274,9 +268,8 @@ def tile_fluxgnn1dlatent_pb_t_kernel(tc, edge_hid, u, enc, W2, b2, W3, b3, out):
         s_inv = const.tile([P, 1], F32)
         weight = const.tile([P, LATENT_TILES], F32)
         u_gain = const.tile([P, 1], F32)
-        u_term = const.tile([N_GROUPS, CELLS_PER_GROUP], F32)
-        u_last_term = const.tile([GRIDS_PER_GROUP, CELLS], F32)
-        g_sum = psum_g.tile([P, GROUP], F32)
+        u_term = const.tile([GRIDS, CELLS], F32)
+        g_sum = psum_g.tile([P, FACES], F32)
 
         transpose_edge(0, 0, psum_tp, "tp")
         copy_edge(0, 0, on_scalar)
@@ -363,43 +356,12 @@ def tile_fluxgnn1dlatent_pb_t_kernel(tc, edge_hid, u, enc, W2, b2, W3, b3, out):
             layer2_sum(LAST, j)
         for chain in range(CHAINS):
             reduce_group(LAST - 1, chain)
-        g_last = psum_tp.tile([P, FACES], F32, tag="tp")
-        for chain in range(CHAINS):
-            for grid, cols in enumerate(HALVES):
-                reduce_partitions(
-                    g_last,
-                    grid,
-                    sums[(LAST, chain)][:, cols],
-                    start=(chain == 0 and grid == 0),
-                    stop=(chain == CHAINS - 1 and grid == GRIDS_PER_GROUP - 1),
-                )
-        nc.vector.tensor_scalar_mul(out=u_term[:], in0=u_bf[:], scalar1=u_gain[0:N_GROUPS, 0:1])
-        nc.vector.tensor_scalar_mul(out=u_last_term[:], in0=u_last[:], scalar1=u_gain[0:GRIDS_PER_GROUP, 0:1])
+        for chain in reversed(range(CHAINS)):
+            reduce_group(LAST, chain)
 
-        faces = g_sum[0:LAST, :].rearrange("g (r f) -> g r f", f=FACES)
-        left = const.tile([LAST, CELLS_PER_GROUP], F32)
-        nc.vector.tensor_tensor(
-            out=left[:].rearrange("g (r c) -> g r c", c=CELLS),
-            in0=u_term[0:LAST, :].rearrange("g (r c) -> g r c", c=CELLS),
-            in1=faces[:, :, 0:CELLS],
-            op=ALU.add,
-        )
-        result = const.tile([LAST, CELLS_PER_GROUP], F32)
-        nc.vector.tensor_tensor(
-            out=result[:].rearrange("g (r c) -> g r c", c=CELLS),
-            in0=left[:].rearrange("g (r c) -> g r c", c=CELLS),
-            in1=faces[:, :, 1:FACES],
-            op=ALU.subtract,
-        )
-        nc.sync.dma_start(
-            out=out[0 : LAST * GRIDS_PER_GROUP, :].rearrange("(g r) c -> g (r c)", r=GRIDS_PER_GROUP), in_=result[:]
-        )
-        left_last = const.tile([GRIDS_PER_GROUP, CELLS], F32)
-        nc.vector.tensor_tensor(
-            out=left_last[:], in0=u_last_term[:], in1=g_last[0:GRIDS_PER_GROUP, 0:CELLS], op=ALU.add
-        )
-        result_last = const.tile([GRIDS_PER_GROUP, CELLS], F32)
-        nc.vector.tensor_tensor(
-            out=result_last[:], in0=left_last[:], in1=g_last[0:GRIDS_PER_GROUP, 1:FACES], op=ALU.subtract
-        )
-        nc.sync.dma_start(out=out[GRIDS - GRIDS_PER_GROUP : GRIDS, :], in_=result_last[:])
+        nc.vector.tensor_scalar_mul(out=u_term[:], in0=u_bf[:], scalar1=u_gain[0:GRIDS, 0:1])
+        left = const.tile([GRIDS, CELLS], F32)
+        nc.vector.tensor_tensor(out=left[:], in0=u_term[:], in1=g_sum[0:GRIDS, 0:CELLS], op=ALU.add)
+        result = const.tile([GRIDS, CELLS], F32)
+        nc.vector.tensor_tensor(out=result[:], in0=left[:], in1=g_sum[0:GRIDS, 1:FACES], op=ALU.subtract)
+        nc.sync.dma_start(out=out, in_=result[:])

from contextlib import ExitStack

import concourse.mybir as mybir
from concourse.masks import make_identity

F32 = mybir.dt.float32
BF16 = mybir.dt.bfloat16
U32 = mybir.dt.uint32
U8 = mybir.dt.uint8
FP8X4 = mybir.dt.float8_e4m3fn_x4
ACT = mybir.ActivationFunctionType
ALU = mybir.AluOpType
AXIS = mybir.AxisListType

P = 128
PACK = 4
GRIDS = 16
FACES = 256
CELLS = FACES - 1
HID = 512
LATENT = 1024
GROUP = 512
N_GROUPS = GRIDS * FACES // GROUP
GRIDS_PER_GROUP = GROUP // FACES
HID_TILES = HID // P
LATENT_TILES = LATENT // P
CHAINS = 2
TANH_BUFS = 12
Z_BANKS = 5
ROWS = FACES // P
BOTH = slice(0, GRIDS_PER_GROUP)
HALF = GROUP // 2
W2_PARTS = 2
W2_PART = HID // W2_PARTS
W3_PARTS = 4
W3_PART = LATENT // W3_PARTS
LAST = N_GROUPS - 1
FLUX_WEIGHT = 0.125
B2_ROW = 0
B3_ROW = B2_ROW + HID_TILES
ENC_ROW = B3_ROW + LATENT_TILES
VEC_ROWS = ENC_ROW + LATENT_TILES

FLOPS = 2 * GRIDS * FACES * HID * (HID + LATENT)


def regroup(copy, grouped, planes):
    copy(
        out=grouped.rearrange("p (c i t) -> p c t i", i=4, t=PACK),
        in_=planes.rearrange("p t (c i) -> p c t i", i=4),
    )


def quantise(nc, codes, scales, grouped):
    nc.vector.quantize_mx(out=codes.bitcast(FP8X4), scales=scales, in_=grouped)


def tile_fluxgnn1dlatent_pb_t_kernel(tc, edge_hid, u, enc, W2, b2, W3, b3, out):
    nc = tc.nc
    with ExitStack() as stack:
        const = stack.enter_context(tc.tile_pool(name="const", bufs=1))
        edge_pool = stack.enter_context(tc.tile_pool(name="edge", bufs=N_GROUPS))
        stage = stack.enter_context(tc.tile_pool(name="stage", bufs=2))
        tanh_pool = stack.enter_context(tc.tile_pool(name="tanh", bufs=TANH_BUFS))
        psum_tp = stack.enter_context(tc.psum_pool(name="psum_tp", bufs=2))
        psum_z = stack.enter_context(tc.psum_pool(name="psum_z", bufs=Z_BANKS))
        psum_g = stack.enter_context(tc.psum_pool(name="psum_g", bufs=1))
        stack.enter_context(tc.manual_schedule())

        vec_rows = const.tile([P, P], BF16)
        nc.gpsimd.memset(vec_rows[:], 0.0)
        edge_view = edge_hid.rearrange("b (p s) k -> p b (s k)", s=ROWS)
        edge_tiles = []
        for g in range(N_GROUPS):
            edge_rows = edge_pool.tile([P, GRIDS_PER_GROUP, ROWS * HID], BF16, tag="edge")
            edge_tiles.append(edge_rows)

        def load_edge(g, grids):
            first = g * GRIDS_PER_GROUP
            nc.sync.dma_start(
                out=edge_tiles[g][:, grids, :], in_=edge_view[:, first + grids.start : first + grids.stop, :]
            )

        w2_planes = const.tile([P, PACK, HID], BF16)
        w3_planes = const.tile([P, PACK, LATENT], BF16)
        w3_view = W3.rearrange("(t p) c -> p t c", p=P)
        load_edge(0, slice(0, 1))
        nc.sync.dma_start(
            out=w2_planes[:].rearrange("p (h e) c -> p h e c", e=2),
            in_=W2.rearrange("(h p e) c -> p h e c", h=2, e=2),
        )
        nc.sync.dma_start(out=vec_rows[B2_ROW:B3_ROW, :], in_=b2.rearrange("(t p) -> t p", p=P))
        nc.sync.dma_start(out=vec_rows[B3_ROW:ENC_ROW, :], in_=b3.rearrange("(t p) -> t p", p=P))
        nc.sync.dma_start(out=vec_rows[ENC_ROW:VEC_ROWS, :], in_=enc.rearrange("(t p) -> t p", p=P))
        load_edge(0, slice(1, 2))
        load_edge(1, BOTH)
        for c in range(0, LATENT, LATENT // 2):
            nc.sync.dma_start(out=w3_planes[:, :, c : c + LATENT // 2], in_=w3_view[:, :, c : c + LATENT // 2])
            if c == 0:
                load_edge(2, BOTH)
        for g in range(3, N_GROUPS):
            load_edge(g, BOTH)
        u_bf = const.tile([GRIDS, CELLS], BF16)
        nc.sync.dma_start(out=u_bf[:], in_=u)

        ident_bf = const.tile([P, P], BF16)
        make_identity(nc, ident_bf[:])
        ident_f32 = const.tile([P, P], F32)
        make_identity(nc, ident_f32[:])
        ones = const.tile([P, P], F32)
        nc.vector.memset(ones[:], 1.0)
        window = const.tile([P, 2 * P], F32)
        nc.vector.memset(window[:], 0.0)
        nc.vector.memset(window[:, P : P + 1], 1.0)
        warm = const.tile([P, 1], F32)
        nc.scalar.activation(out=warm[:], in_=ones[:, 0:1], func=ACT.Gelu)

        w2_grouped = const.tile([P, HID * PACK], BF16, align_bytes=64)
        w2_codes = const.tile([P, HID], U32, align_bytes=64)
        w2_scales = const.tile([P, HID], U8, align_bytes=64)
        w3_grouped = const.tile([P, LATENT * PACK], BF16, align_bytes=64)
        w3_codes = const.tile([P, LATENT], U32, align_bytes=64)
        w3_scales = const.tile([P, LATENT], U8, align_bytes=64)

        transposed = {}
        edge_grouped = {}
        edge_codes = {}
        x_planes = {}
        x_grouped = {}
        x_codes = {}
        sums = {}
        fluxes = {}
        ALL = slice(0, GROUP)
        HALVES = (slice(0, HALF), slice(HALF, GROUP))

        def packed(cols):
            return slice(cols.start * PACK, cols.stop * PACK)

        def transpose_edge(g, half, pool, tag):
            words = edge_tiles[g][:, half, :].bitcast(F32)
            tp = pool.tile([P, 2, HALF], F32, tag=tag)
            for s in range(ROWS):
                for h in range(2):
                    first = s * (HID // 2) + h * P
                    nc.tensor.transpose(tp[:, h, s * P : (s + 1) * P], words[:, first : first + P], ident_f32[:])
            transposed[(g, half)] = tp

        def copy_edge(g, half, copy):
            if half == 0:
                grouped = stage.tile([P, GROUP * PACK], BF16, tag="edge_grouped", align_bytes=64)
                edge_grouped[g] = grouped
            grouped_words = edge_grouped[g][:, packed(HALVES[half])].bitcast(F32)
            copy(
                out=grouped_words.rearrange("p (r s h) -> p r s h", s=ROWS, h=2),
                in_=transposed[(g, half)][:].rearrange("p h (s r) -> p r s h", s=ROWS),
            )

        def quantise_edge(g, cols):
            if cols.start == 0:
                codes = stage.tile([P, GROUP], U32, tag="edge_codes", align_bytes=64)
                scales = stage.tile([P, GROUP], U8, tag="edge_scales", align_bytes=64)
                edge_codes[g] = (codes, scales)
            codes, scales = edge_codes[g]
            quantise(nc, codes[:, cols], scales[:, cols], edge_grouped[g][:, packed(cols)])

        def multiply(weights, tile, moving, cols):
            channels = slice(tile * P, (tile + 1) * P)
            z = psum_z.tile([P, cols.stop - cols.start], F32, tag="z")
            nc.tensor.matmul_mx(
                out=z[:],
                lhsT=weights[0][:, channels].bitcast(FP8X4),
                lhsT_scale=weights[1][:, channels],
                rhs=moving[0][:, cols].bitcast(FP8X4),
                rhs_scale=moving[1][:, cols],
                start=True,
                stop=True,
            )
            return z

        def layer1(g, tiles, cols):
            if g not in x_planes:
                planes = stage.tile([P, PACK, GROUP], BF16, tag="x_planes")
                x_planes[g] = planes
            for t in tiles:
                z = multiply((w2_codes, w2_scales), t, edge_codes[g], cols)
                nc.scalar.activation(
                    out=x_planes[g][:, t, cols], in_=z[:], func=ACT.Gelu, bias=vec_cols[:, B2_ROW + t : B2_ROW + t + 1]
                )

        def regroup_x(g, cols):
            if cols.start == 0:
                grouped = stage.tile([P, GROUP * PACK], BF16, tag="x_grouped", align_bytes=64)
                x_grouped[g] = grouped
            regroup(nc.vector.tensor_copy, x_grouped[g][:, packed(cols)], x_planes[g][:, :, cols])

        def quantise_x(g, cols):
            if cols.start == 0:
                codes = stage.tile([P, GROUP], U32, tag="x_codes", align_bytes=64)
                scales = stage.tile([P, GROUP], U8, tag="x_scales", align_bytes=64)
                x_codes[g] = (codes, scales)
            codes, scales = x_codes[g]
            quantise(nc, codes[:, cols], scales[:, cols], x_grouped[g][:, packed(cols)])

        def layer2_tanh(g, j):
            z = multiply((w3_codes, w3_scales), j, x_codes[g], ALL)
            flux = tanh_pool.tile([P, GROUP], F32, tag="flux")
            nc.scalar.activation(
                out=flux[:], in_=z[:], func=ACT.Tanh, bias=vec_cols[:, B3_ROW + j : B3_ROW + j + 1]
            )
            fluxes[(g, j)] = flux

        def layer2_sum(g, j):
            flux = fluxes[(g, j)]
            if j < CHAINS:
                partial = stage.tile([P, GROUP], F32, tag="sum%d" % j)
                nc.vector.tensor_scalar_mul(out=partial[:], in0=flux[:], scalar1=weight[:, j : j + 1])
                sums[(g, j)] = partial
            else:
                partial = sums[(g, (j - 1 if (g, j) == (LAST, LATENT_TILES - 1) else j) % CHAINS)]
                nc.vector.scalar_tensor_tensor(
                    out=partial[:],
                    in0=flux[:],
                    scalar=weight[:, j : j + 1],
                    in1=partial[:],
                    op0=ALU.mult,
                    op1=ALU.add,
                )

        def reduce_group(g, chain):
            for grid, cols in enumerate(HALVES):
                b = g * GRIDS_PER_GROUP + grid
                nc.tensor.matmul(
                    out=g_sum[:],
                    lhsT=window[:, P - b : 2 * P - b],
                    rhs=sums[(g, chain)][:, cols],
                    start=(b == 0 and chain == 0),
                    stop=(b == GRIDS - 1 and chain == 0),
                )

        def regroup_w(copy, grouped, planes, part, width):
            cols = slice(part * width, (part + 1) * width)
            regroup(copy, grouped[:, packed(cols)], planes[:, :, cols])

        def quantise_w(codes, scales, grouped, part, width):
            cols = slice(part * width, (part + 1) * width)
            quantise(nc, codes[:, cols], scales[:, cols], grouped[:, packed(cols)])

        def regroup_w2(part, copy):
            regroup_w(copy, w2_grouped, w2_planes, part, W2_PART)

        def quantise_w2(part):
            quantise_w(w2_codes, w2_scales, w2_grouped, part, W2_PART)

        def regroup_w3(part):
            regroup_w(nc.vector.tensor_copy, w3_grouped, w3_planes, part, W3_PART)

        def quantise_w3(part):
            quantise_w(w3_codes, w3_scales, w3_grouped, part, W3_PART)

        on_vector = nc.vector.tensor_copy
        on_scalar = nc.scalar.copy

        vec_cols = const.tile([P, VEC_ROWS], F32)
        enc_cols = vec_cols[:, ENC_ROW:VEC_ROWS]
        enc_sq = const.tile([P, LATENT_TILES], F32)
        s_sum = const.tile([P, 1], F32)
        s_eps = const.tile([P, 1], F32)
        s_inv = const.tile([P, 1], F32)
        weight = const.tile([P, LATENT_TILES], F32)
        u_gain = const.tile([P, 1], F32)
        u_term = const.tile([GRIDS, CELLS], F32)
        g_sum = psum_g.tile([P, FACES], F32)

        transpose_edge(0, 0, psum_tp, "tp")
        copy_edge(0, 0, on_scalar)
        regroup_w2(0, on_vector)
        regroup_w2(1, on_scalar)
        vec_ps = psum_z.tile([P, P], BF16, tag="z")
        nc.tensor.transpose(vec_ps[:], vec_rows[:], ident_bf[:])
        transpose_edge(0, 1, psum_tp, "tp")
        nc.vector.tensor_copy(out=vec_cols[:], in_=vec_ps[:, 0:VEC_ROWS])
        quantise_edge(0, HALVES[0])
        nc.vector.tensor_tensor(out=enc_sq[:], in0=enc_cols, in1=enc_cols, op=ALU.mult)
        quantise_w2(0)
        s_ps = psum_z.tile([P, LATENT_TILES], F32, tag="z")
        nc.tensor.matmul(out=s_ps[:], lhsT=ones[:], rhs=enc_sq[:], start=True, stop=True)
        nc.vector.reduce_sum(out=s_sum[:], in_=s_ps[:], axis=AXIS.X)
        copy_edge(0, 1, on_scalar)
        layer1(0, (0, 1), HALVES[0])
        quantise_w2(1)
        nc.vector.tensor_scalar_add(out=s_eps[:], in0=s_sum[:], scalar1=1e-12)
        quantise_edge(0, HALVES[1])
        nc.vector.reciprocal(out=s_inv[:], in_=s_eps[:])
        layer1(0, (2, 3), HALVES[0])
        transpose_edge(1, 0, psum_z, "z")
        copy_edge(1, 0, on_scalar)
        transpose_edge(1, 1, psum_tp, "tp")
        regroup_w3(0)
        regroup_w3(1)
        layer1(0, range(HID_TILES), HALVES[1])
        copy_edge(1, 1, on_vector)
        quantise_w3(0)
        quantise_edge(1, ALL)
        transpose_edge(2, 0, psum_tp, "tp")
        copy_edge(2, 0, on_scalar)
        regroup_x(0, HALVES[0])
        layer1(1, range(HID_TILES), ALL)
        regroup_x(0, HALVES[1])
        quantise_x(0, HALVES[0])
        nc.vector.tensor_scalar(
            out=weight[:], in0=enc_cols, scalar1=s_inv[:, 0:1], scalar2=FLUX_WEIGHT, op0=ALU.mult, op1=ALU.mult
        )
        nc.vector.tensor_tensor(out=u_gain[:], in0=s_sum[:], in1=s_inv[:], op=ALU.mult)
        quantise_x(0, HALVES[1])
        for j in range(2):
            layer2_tanh(0, j)
        transpose_edge(2, 1, psum_tp, "tp")
        copy_edge(2, 1, on_scalar)
        regroup_w3(2)
        quantise_w3(1)
        quantise_w3(2)
        for j in range(2, 6):
            layer2_tanh(0, j)
        regroup_w3(3)
        layer2_sum(0, 0)
        quantise_w3(3)
        layer2_sum(0, 1)
        for j in range(6, LATENT_TILES):
            layer2_tanh(0, j)
        quantise_edge(2, ALL)
        regroup_x(1, ALL)
        layer2_sum(0, 2)
        quantise_x(1, ALL)
        for j in range(3, LATENT_TILES):
            layer2_sum(0, j)

        for g in range(1, LAST):
            layer1(g + 1, range(HID_TILES), ALL)
            if g + 2 < N_GROUPS:
                for half, copy in enumerate((on_vector, on_scalar)):
                    transpose_edge(g + 2, half, psum_tp, "tp")
                    copy_edge(g + 2, half, copy)
            regroup_x(g + 1, ALL)
            if g + 2 < N_GROUPS:
                quantise_edge(g + 2, ALL)
            for j in range(LATENT_TILES):
                if j == CHAINS:
                    quantise_x(g + 1, ALL)
                layer2_tanh(g, j)
                layer2_sum(g, j)
                if j in (3, 5):
                    reduce_group(g - 1, j // 2 - 1)

        for j in range(LATENT_TILES):
            layer2_tanh(LAST, j)
            layer2_sum(LAST, j)
        for chain in range(CHAINS):
            reduce_group(LAST - 1, chain)
        for chain in reversed(range(CHAINS)):
            reduce_group(LAST, chain)

        nc.vector.tensor_scalar_mul(out=u_term[:], in0=u_bf[:], scalar1=u_gain[0:GRIDS, 0:1])
        left = const.tile([GRIDS, CELLS], F32)
        nc.vector.tensor_tensor(out=left[:], in0=u_term[:], in1=g_sum[0:GRIDS, 0:CELLS], op=ALU.add)
        result = const.tile([GRIDS, CELLS], F32)
        nc.vector.tensor_tensor(out=result[:], in0=left[:], in1=g_sum[0:GRIDS, 1:FACES], op=ALU.subtract)
        nc.sync.dma_start(out=out, in_=result[:])
